import numpy as np
import ml_dtypes


def mxq(x, axis, fmt="e4m3"):
    dtype, down = {"e4m3": (ml_dtypes.float8_e4m3fn, 7), "e5m2": (ml_dtypes.float8_e5m2, 14)}[fmt]
    v = np.moveaxis(np.asarray(x, np.float32).astype(ml_dtypes.bfloat16).astype(np.float64), axis, -1)
    blocks = v.reshape(v.shape[:-1] + (-1, 32))
    amax = np.abs(blocks).max(-1, keepdims=True)
    byte = np.maximum(np.where(amax > 0, np.frexp(amax)[1] - 1 + 127, 0) - down, 1)
    scale = np.exp2(byte - 127.0)
    codes = (blocks / scale).astype(np.float32).astype(dtype).astype(np.float64)
    return np.moveaxis((codes * scale).reshape(v.shape), -1, axis)


WIDE = False


def mx_kscale(k):
    if not WIDE:
        return np.ones(k)
    levels = np.array([10, -10, 5, -5, 0])
    a = np.random.permutation(np.resize(levels, k // 512 * 4)).reshape(k // 512, 4)
    idx = np.arange(k)
    return np.exp2(a[idx // 512, idx % 128 // 32])


BF16 = ml_dtypes.bfloat16


def bf(x):
    return np.asarray(x, np.float32).astype(BF16)


def f64(x):
    return np.asarray(x).astype(np.float64)


B, N, D, HEAD, HALF = 1, 1024, 512, 1024, 512
E = HEAD + HALF + HALF
EPS_RMS = 1e-6
EPS_NORM = 1e-12


def setup_inputs():
    s = mx_kscale(D)
    return {"x": bf(np.random.standard_normal((B, N, D))),
            "g": bf((1.0 + 0.1 * np.random.standard_normal(D)) * s),
            "W1": bf(np.random.standard_normal((D, E)) / np.sqrt(D) / s[:, None]),
            "b1": bf(np.random.standard_normal(E) * 0.3)}


def reference(x, g, W1, b1):
    x = f64(x)
    xn = x * (1.0 / np.sqrt(np.mean(np.square(x), axis=-1, keepdims=True) + EPS_RMS)) * f64(g)
    pre = (mxq(xn, 2, "e4m3") @ mxq(f64(W1), 0, "e4m3")) + f64(b1)
    enriched = np.square(np.maximum(pre, 0.0))
    head = enriched[..., :HEAD]
    x_left = enriched[..., HEAD:HEAD + HALF]
    x_right = enriched[..., HEAD + HALF:]
    nrm = np.sqrt(np.sum(np.square(x_right), axis=-1, keepdims=True))
    xr_n = x_right / np.maximum(nrm, EPS_NORM)
    return head, x_left, xr_n

@@ -1,0 +1,200 @@
+from contextlib import ExitStack
+
+import concourse.masks as masks
+import concourse.mybir as mybir
+
+F32 = mybir.dt.float32
+BF16 = mybir.dt.bfloat16
+U32 = mybir.dt.uint32
+U8 = mybir.dt.uint8
+FP8X4 = mybir.dt.float8_e4m3fn_x4
+ACT = mybir.ActivationFunctionType
+ALU = mybir.AluOpType
+
+P = 128
+PACK = 4
+TOKENS = 1024
+D = 512
+HEAD = 1024
+HALF = 512
+E = HEAD + HALF + HALF
+BANK = 512
+TOK_TILES = TOKENS // P
+PAIRS = TOK_TILES // 2
+EPS_RMS = 1e-6
+EPS_NORM = 1e-12
+FLT_MAX = 3.4028234663852886e38
+
+FLOPS = 2 * TOKENS * D * E
+
+
+def tile_avey_pa_kernel(tc, x, g, W1, b1, out_0, out_1, out_2):
+    nc = tc.nc
+
+    x_rows = x.flatten_outer_dims().rearrange("(p i) k -> p i k", i=TOK_TILES)
+    head_rows = out_0.flatten_outer_dims().rearrange("(p i) f -> p i f", i=TOK_TILES)
+    left_rows = out_1.flatten_outer_dims().rearrange("(p i) f -> p i f", i=TOK_TILES)
+    right_rows = out_2.flatten_outer_dims().rearrange("(p i) f -> p i f", i=TOK_TILES)
+    w_rows = W1.rearrange("(t p) f -> p t f", p=P)
+
+    pieces = (
+        (right_rows, HEAD + HALF, HALF),
+        (left_rows, HEAD, HALF),
+        (head_rows, 0, HEAD),
+    )
+    bank_order = [first // BANK + b for (rows, first, width) in pieces for b in range(width // BANK)]
+
+    with ExitStack() as ctx:
+        keep = ctx.enter_context(tc.tile_pool(name="keep", bufs=1))
+        stage = ctx.enter_context(tc.tile_pool(name="stage", bufs=2))
+        flow = ctx.enter_context(tc.tile_pool(name="flow", bufs=3))
+        psum_gain = ctx.enter_context(tc.psum_pool(name="psum_gain", bufs=1))
+        psum_turn = ctx.enter_context(tc.psum_pool(name="psum_turn", bufs=2))
+        psum_acc = ctx.enter_context(tc.psum_pool(name="psum_acc", bufs=5))
+
+        warm = keep.tile([P, 1], F32)
+        nc.vector.memset(warm[:], 1.0)
+        nc.scalar.activation(out=warm[:], in_=warm[:], func=ACT.Sqrt)
+
+        ident = keep.tile([P, P], BF16)
+        masks.make_identity(nc, ident[:])
+        ones = keep.tile([P, P], BF16)
+        nc.vector.memset(ones[:], 1.0)
+
+        g_row = keep.tile([P, D], BF16)
+        nc.vector.memset(g_row[:], 0.0)
+        nc.scalar.dma_start(out=g_row[0:1, :], in_=g.unsqueeze(0))
+        b_row = keep.tile([P, E], BF16)
+        nc.vector.memset(b_row[:], 0.0)
+        nc.scalar.dma_start(out=b_row[0:1, :], in_=b1.unsqueeze(0))
+
+        x_sb = keep.tile([P, TOK_TILES, D], BF16)
+        for j in range(PAIRS):
+            nc.sync.dma_start(out=x_sb[:, 2 * j : 2 * j + 2, :], in_=x_rows[:, 2 * j : 2 * j + 2, :])
+        w_raw = keep.tile([P, PACK, E], BF16)
+        for b in bank_order:
+            cols = slice(b * BANK, (b + 1) * BANK)
+            nc.sync.dma_start(out=w_raw[:, :, cols], in_=w_rows[:, :, cols])
+
+        gain = psum_gain.tile([P, D], F32)
+        nc.tensor.matmul(out=gain[:], lhsT=ones[:], rhs=g_row[:], start=True, stop=True)
+        bias = keep.tile([P, E], F32)
+        for b in bank_order:
+            cols = slice(b * BANK, (b + 1) * BANK)
+            acc = psum_acc.tile([P, BANK], F32, tag="acc")
+            nc.tensor.matmul(out=acc[:], lhsT=ones[:], rhs=b_row[:, cols], start=True, stop=True)
+            nc.vector.tensor_copy(out=bias[:, cols], in_=acc[:])
+
+        x_codes = keep.tile([P, TOKENS], U32, align_bytes=64)
+        x_scales = keep.tile([P, TOKENS], U8, align_bytes=64)
+        w_codes = keep.tile([P, E], U32, align_bytes=64)
+        w_scales = keep.tile([P, E], U8, align_bytes=64)
+
+        squares = keep.tile([P, TOK_TILES, D], BF16)
+        sumsq = keep.tile([P, TOK_TILES], F32)
+        rms = keep.tile([P, TOK_TILES], F32)
+        rstd = keep.tile([P, TOK_TILES], F32)
+
+        def normalise_pair(j):
+            pair = slice(2 * j, 2 * j + 2)
+            for i in (2 * j, 2 * j + 1):
+                nc.scalar.activation(
+                    out=squares[:, i, :], in_=x_sb[:, i, :], func=ACT.Square, accum_out=sumsq[:, i : i + 1]
+                )
+            nc.scalar.activation(out=rms[:, pair], in_=sumsq[:, pair], func=ACT.Sqrt, bias=EPS_RMS, scale=1.0 / D)
+            nc.vector.reciprocal(out=rstd[:, pair], in_=rms[:, pair])
+            xn = stage.tile([P, 2, D], BF16)
+            for h in range(2):
+                i = 2 * j + h
+                nc.vector.scalar_tensor_tensor(
+                    out=xn[:, h, :],
+                    in0=x_sb[:, i, :],
+                    scalar=rstd[:, i : i + 1],
+                    in1=gain[:],
+                    op0=ALU.mult,
+                    op1=ALU.mult,
+                )
+            turned = psum_turn.tile([P, 2, PACK, P], BF16)
+            for h in range(2):
+                for t in range(PACK):
+                    nc.tensor.transpose(turned[:, h, t, :], xn[:, h, t * P : (t + 1) * P], ident[:])
+            x_grouped = stage.tile([P, 2, P, PACK], BF16, align_bytes=64)
+            nc.scalar.copy(out=x_grouped[:], in_=turned[:].rearrange("p h t r -> p h r t"))
+            toks = slice(2 * j * P, (2 * j + 2) * P)
+            nc.vector.quantize_mx(
+                out=x_codes[:, toks].bitcast(FP8X4),
+                scales=x_scales[:, toks],
+                in_=x_grouped[:].rearrange("p h r t -> p (h r t)"),
+            )
+
+        def quantise_w_bank(b):
+            cols = slice(b * BANK, (b + 1) * BANK)
+            w_grouped = stage.tile([P, BANK, PACK], BF16, align_bytes=64)
+            nc.vector.tensor_copy(
+                out=w_grouped[:].rearrange("p (c i) t -> p c t i", i=4),
+                in_=w_raw[:, :, cols].rearrange("p t (c i) -> p c t i", i=4),
+            )
+            nc.vector.quantize_mx(
+                out=w_codes[:, cols].bitcast(FP8X4),
+                scales=w_scales[:, cols],
+                in_=w_grouped[:].rearrange("p f t -> p (f t)"),
+            )
+
+        norm2 = keep.tile([P, TOK_TILES], F32)
+        norm2_floor = keep.tile([P, TOK_TILES], F32)
+        norm = keep.tile([P, TOK_TILES], F32)
+        inv_norm = keep.tile([P, TOK_TILES], F32)
+
+        def enrich_tile(i):
+            toks = slice(i * P, (i + 1) * P)
+            one = slice(i, i + 1)
+            pre = flow.tile([P, E], F32)
+            enriched = flow.tile([P, E], F32)
+            for rows, first, width in pieces:
+                span = slice(first, first + width)
+                for b in range(first // BANK, (first + width) // BANK):
+                    cols = slice(b * BANK, (b + 1) * BANK)
+                    acc = psum_acc.tile([P, BANK], F32, tag="acc")
+                    nc.tensor.matmul_mx(
+                        out=acc[:],
+                        lhsT=x_codes[:, toks].bitcast(FP8X4),
+                        lhsT_scale=x_scales[:, toks],
+                        rhs=w_codes[:, cols].bitcast(FP8X4),
+                        rhs_scale=w_scales[:, cols],
+                        start=True,
+                        stop=True,
+                    )
+                    nc.vector.tensor_tensor(out=pre[:, cols], in0=acc[:], in1=bias[:, cols], op=ALU.add)
+                nc.gpsimd.tensor_scalar(
+                    out=pre[:, span], in0=pre[:, span], scalar1=FLT_MAX, scalar2=0.0, op0=ALU.min, op1=ALU.max
+                )
+                nc.scalar.activation(out=enriched[:, span], in_=pre[:, span], func=ACT.Square)
+                if rows is right_rows:
+                    fourth = flow.tile([P, HALF], BF16)
+                    nc.scalar.activation(
+                        out=fourth[:], in_=enriched[:, span], func=ACT.Square, accum_out=norm2[:, one]
+                    )
+                    nc.vector.tensor_scalar_max(out=norm2_floor[:, one], in0=norm2[:, one], scalar1=EPS_NORM * EPS_NORM)
+                    nc.scalar.activation(out=norm[:, one], in_=norm2_floor[:, one], func=ACT.Sqrt)
+                    nc.vector.reciprocal(out=inv_norm[:, one], in_=norm[:, one])
+                    unit = flow.tile([P, HALF], F32)
+                    nc.gpsimd.tensor_scalar(
+                        out=unit[:],
+                        in0=enriched[:, span],
+                        scalar1=inv_norm[:, one],
+                        scalar2=1.0,
+                        op0=ALU.mult,
+                        op1=ALU.mult,
+                    )
+                    nc.sync.dma_start(out=rows[:, i, :], in_=unit[:])
+                else:
+                    nc.sync.dma_start(out=rows[:, i, :], in_=enriched[:, span])
+
+        normalise_pair(0)
+        for b in bank_order:
+            quantise_w_bank(b)
+        for j in range(PAIRS):
+            if j + 1 < PAIRS:
+                normalise_pair(j + 1)
+            enrich_tile(2 * j)
+            enrich_tile(2 * j + 1)

@@ -20,7 +20,8 @@ HALF = 512
 E = HEAD + HALF + HALF
 BANK = 512
 TOK_TILES = TOKENS // P
-PAIRS = TOK_TILES // 2
+BANKS = E // BANK
+UNITS = TOK_TILES * BANKS
 EPS_RMS = 1e-6
 EPS_NORM = 1e-12
 FLT_MAX = 3.4028234663852886e38
@@ -31,35 +32,31 @@ FLOPS = 2 * TOKENS * D * E
 def tile_avey_pa_kernel(tc, x, g, W1, b1, out_0, out_1, out_2):
     nc = tc.nc
 
-    x_rows = x.flatten_outer_dims().rearrange("(p i) k -> p i k", i=TOK_TILES)
-    head_rows = out_0.flatten_outer_dims().rearrange("(p i) f -> p i f", i=TOK_TILES)
-    left_rows = out_1.flatten_outer_dims().rearrange("(p i) f -> p i f", i=TOK_TILES)
-    right_rows = out_2.flatten_outer_dims().rearrange("(p i) f -> p i f", i=TOK_TILES)
-    w_rows = W1.rearrange("(t p) f -> p t f", p=P)
+    x_rows = x.flatten_outer_dims().rearrange("(p t) k -> p t k", t=TOK_TILES)
+    head_rows = out_0.flatten_outer_dims().rearrange("(p t) f -> p t f", t=TOK_TILES)
+    left_rows = out_1.flatten_outer_dims().rearrange("(p t) f -> p t f", t=TOK_TILES)
+    right_rows = out_2.flatten_outer_dims().rearrange("(p t) f -> p t f", t=TOK_TILES)
+    w_rows = W1.rearrange("(j p) f -> p j f", p=P)
 
-    pieces = (
-        (right_rows, HEAD + HALF, HALF),
-        (left_rows, HEAD, HALF),
-        (head_rows, 0, HEAD),
+    banks = (
+        (HEAD + HALF, right_rows),
+        (HEAD, left_rows),
+        (0, head_rows[:, :, 0:BANK]),
+        (BANK, head_rows[:, :, BANK:HEAD]),
     )
-    bank_order = [first // BANK + b for (rows, first, width) in pieces for b in range(width // BANK)]
 
     with ExitStack() as ctx:
+        ctx.enter_context(tc.manual_schedule())
         keep = ctx.enter_context(tc.tile_pool(name="keep", bufs=1))
         stage = ctx.enter_context(tc.tile_pool(name="stage", bufs=2))
-        flow = ctx.enter_context(tc.tile_pool(name="flow", bufs=3))
+        flow = ctx.enter_context(tc.tile_pool(name="flow", bufs=6))
         psum_gain = ctx.enter_context(tc.psum_pool(name="psum_gain", bufs=1))
-        psum_turn = ctx.enter_context(tc.psum_pool(name="psum_turn", bufs=2))
-        psum_acc = ctx.enter_context(tc.psum_pool(name="psum_acc", bufs=5))
+        psum_turn = ctx.enter_context(tc.psum_pool(name="psum_turn", bufs=1))
+        psum_acc = ctx.enter_context(tc.psum_pool(name="psum_acc", bufs=6))
 
         warm = keep.tile([P, 1], F32)
         nc.vector.memset(warm[:], 1.0)
-        nc.scalar.activation(out=warm[:], in_=warm[:], func=ACT.Sqrt)
-
-        ident = keep.tile([P, P], BF16)
-        masks.make_identity(nc, ident[:])
-        ones = keep.tile([P, P], BF16)
-        nc.vector.memset(ones[:], 1.0)
+        nc.scalar.activation(out=warm[:], in_=warm[:], func=ACT.Square)
 
         g_row = keep.tile([P, D], BF16)
         nc.vector.memset(g_row[:], 0.0)
@@ -67,23 +64,27 @@ def tile_avey_pa_kernel(tc, x, g, W1, b1, out_0, out_1, out_2):
         b_row = keep.tile([P, E], BF16)
         nc.vector.memset(b_row[:], 0.0)
         nc.scalar.dma_start(out=b_row[0:1, :], in_=b1.unsqueeze(0))
+        ones = keep.tile([P, P], BF16)
+        nc.vector.memset(ones[:], 1.0)
+        ident = keep.tile([P, P], BF16)
+        masks.make_identity(nc, ident[:])
+        minus_half = keep.tile([P, 2], F32)
+        nc.gpsimd.memset(minus_half[:], -0.5)
 
         x_sb = keep.tile([P, TOK_TILES, D], BF16)
-        for j in range(PAIRS):
-            nc.sync.dma_start(out=x_sb[:, 2 * j : 2 * j + 2, :], in_=x_rows[:, 2 * j : 2 * j + 2, :])
+        nc.sync.dma_start(out=x_sb[:, 0:2, :], in_=x_rows[:, 0:2, :])
+        nc.sync.dma_start(out=x_sb[:, 2:TOK_TILES, :], in_=x_rows[:, 2:TOK_TILES, :])
         w_raw = keep.tile([P, PACK, E], BF16)
-        for b in bank_order:
-            cols = slice(b * BANK, (b + 1) * BANK)
-            nc.sync.dma_start(out=w_raw[:, :, cols], in_=w_rows[:, :, cols])
+        for first, rows in banks:
+            nc.sync.dma_start(out=w_raw[:, :, first : first + BANK], in_=w_rows[:, :, first : first + BANK])
 
         gain = psum_gain.tile([P, D], F32)
         nc.tensor.matmul(out=gain[:], lhsT=ones[:], rhs=g_row[:], start=True, stop=True)
         bias = keep.tile([P, E], F32)
-        for b in bank_order:
-            cols = slice(b * BANK, (b + 1) * BANK)
-            acc = psum_acc.tile([P, BANK], F32, tag="acc")
-            nc.tensor.matmul(out=acc[:], lhsT=ones[:], rhs=b_row[:, cols], start=True, stop=True)
-            nc.vector.tensor_copy(out=bias[:, cols], in_=acc[:])
+        for first, rows in banks:
+            spread = psum_acc.tile([P, BANK], F32, tag="acc")
+            nc.tensor.matmul(out=spread[:], lhsT=ones[:], rhs=b_row[:, first : first + BANK], start=True, stop=True)
+            nc.vector.tensor_copy(out=bias[:, first : first + BANK], in_=spread[:])
 
         x_codes = keep.tile([P, TOKENS], U32, align_bytes=64)
         x_scales = keep.tile([P, TOKENS], U8, align_bytes=64)
@@ -92,109 +93,121 @@ def tile_avey_pa_kernel(tc, x, g, W1, b1, out_0, out_1, out_2):
 
         squares = keep.tile([P, TOK_TILES, D], BF16)
         sumsq = keep.tile([P, TOK_TILES], F32)
-        rms = keep.tile([P, TOK_TILES], F32)
+        mean_sq = keep.tile([P, TOK_TILES], F32)
         rstd = keep.tile([P, TOK_TILES], F32)
 
-        def normalise_pair(j):
-            pair = slice(2 * j, 2 * j + 2)
-            for i in (2 * j, 2 * j + 1):
+        def rms_statistics(pair):
+            both = slice(2 * pair, 2 * pair + 2)
+            for t in (2 * pair, 2 * pair + 1):
                 nc.scalar.activation(
-                    out=squares[:, i, :], in_=x_sb[:, i, :], func=ACT.Square, accum_out=sumsq[:, i : i + 1]
+                    out=squares[:, t, :], in_=x_sb[:, t, :], func=ACT.Square, accum_out=sumsq[:, t : t + 1]
                 )
-            nc.scalar.activation(out=rms[:, pair], in_=sumsq[:, pair], func=ACT.Sqrt, bias=EPS_RMS, scale=1.0 / D)
-            nc.vector.reciprocal(out=rstd[:, pair], in_=rms[:, pair])
-            xn = stage.tile([P, 2, D], BF16)
-            for h in range(2):
-                i = 2 * j + h
-                nc.vector.scalar_tensor_tensor(
-                    out=xn[:, h, :],
-                    in0=x_sb[:, i, :],
-                    scalar=rstd[:, i : i + 1],
-                    in1=gain[:],
-                    op0=ALU.mult,
-                    op1=ALU.mult,
-                )
-            turned = psum_turn.tile([P, 2, PACK, P], BF16)
-            for h in range(2):
-                for t in range(PACK):
-                    nc.tensor.transpose(turned[:, h, t, :], xn[:, h, t * P : (t + 1) * P], ident[:])
-            x_grouped = stage.tile([P, 2, P, PACK], BF16, align_bytes=64)
-            nc.scalar.copy(out=x_grouped[:], in_=turned[:].rearrange("p h t r -> p h r t"))
-            toks = slice(2 * j * P, (2 * j + 2) * P)
+            nc.gpsimd.tensor_scalar(
+                out=mean_sq[:, both], in0=sumsq[:, both], scalar1=1.0 / D, scalar2=EPS_RMS, op0=ALU.mult, op1=ALU.add
+            )
+            nc.gpsimd.tensor_tensor(out=rstd[:, both], in0=mean_sq[:, both], in1=minus_half[:], op=ALU.pow)
+
+        x_grouped = {}
+
+        def turn(t):
+            xn = stage.tile([P, D], BF16, name="xn")
+            nc.vector.scalar_tensor_tensor(
+                out=xn[:], in0=x_sb[:, t, :], scalar=rstd[:, t : t + 1], in1=gain[:], op0=ALU.mult, op1=ALU.mult
+            )
+            turned = psum_turn.tile([P, PACK, P], BF16, name="turned")
+            for j in range(PACK):
+                nc.tensor.transpose(turned[:, j, :], xn[:, j * P : (j + 1) * P], ident[:])
+            x_grouped[t] = stage.tile([P, P, PACK], BF16, align_bytes=64, name="x_grouped")
+            nc.scalar.copy(out=x_grouped[t][:], in_=turned[:].rearrange("p j r -> p r j"))
+
+        def quantise_x(t):
+            toks = slice(t * P, (t + 1) * P)
             nc.vector.quantize_mx(
                 out=x_codes[:, toks].bitcast(FP8X4),
                 scales=x_scales[:, toks],
-                in_=x_grouped[:].rearrange("p h r t -> p (h r t)"),
+                in_=x_grouped[t][:].rearrange("p r j -> p (r j)"),
             )
 
-        def quantise_w_bank(b):
-            cols = slice(b * BANK, (b + 1) * BANK)
-            w_grouped = stage.tile([P, BANK, PACK], BF16, align_bytes=64)
+        w_grouped = {}
+
+        def regroup_w(q):
+            first = banks[q][0]
+            w_grouped[q] = stage.tile([P, BANK, PACK], BF16, align_bytes=64, name="w_grouped")
             nc.vector.tensor_copy(
-                out=w_grouped[:].rearrange("p (c i) t -> p c t i", i=4),
-                in_=w_raw[:, :, cols].rearrange("p t (c i) -> p c t i", i=4),
+                out=w_grouped[q][:].rearrange("p (c i) j -> p c j i", i=4),
+                in_=w_raw[:, :, first : first + BANK].rearrange("p j (c i) -> p c j i", i=4),
             )
+
+        def quantise_w(q):
+            first = banks[q][0]
             nc.vector.quantize_mx(
-                out=w_codes[:, cols].bitcast(FP8X4),
-                scales=w_scales[:, cols],
-                in_=w_grouped[:].rearrange("p f t -> p (f t)"),
+                out=w_codes[:, first : first + BANK].bitcast(FP8X4),
+                scales=w_scales[:, first : first + BANK],
+                in_=w_grouped[q][:].rearrange("p f j -> p (f j)"),
+            )
+
+        sums = {}
+
+        def multiply(t, q):
+            first = banks[q][0]
+            toks = slice(t * P, (t + 1) * P)
+            sums[q] = psum_acc.tile([P, BANK], F32, tag="acc", name="acc")
+            nc.tensor.matmul_mx(
+                out=sums[q][:],
+                lhsT=x_codes[:, toks].bitcast(FP8X4),
+                lhsT_scale=x_scales[:, toks],
+                rhs=w_codes[:, first : first + BANK].bitcast(FP8X4),
+                rhs_scale=w_scales[:, first : first + BANK],
+                start=True,
+                stop=True,
             )
 
         norm2 = keep.tile([P, TOK_TILES], F32)
         norm2_floor = keep.tile([P, TOK_TILES], F32)
-        norm = keep.tile([P, TOK_TILES], F32)
         inv_norm = keep.tile([P, TOK_TILES], F32)
+        right = {}
 
-        def enrich_tile(i):
-            toks = slice(i * P, (i + 1) * P)
-            one = slice(i, i + 1)
-            pre = flow.tile([P, E], F32)
-            enriched = flow.tile([P, E], F32)
-            for rows, first, width in pieces:
-                span = slice(first, first + width)
-                for b in range(first // BANK, (first + width) // BANK):
-                    cols = slice(b * BANK, (b + 1) * BANK)
-                    acc = psum_acc.tile([P, BANK], F32, tag="acc")
-                    nc.tensor.matmul_mx(
-                        out=acc[:],
-                        lhsT=x_codes[:, toks].bitcast(FP8X4),
-                        lhsT_scale=x_scales[:, toks],
-                        rhs=w_codes[:, cols].bitcast(FP8X4),
-                        rhs_scale=w_scales[:, cols],
-                        start=True,
-                        stop=True,
-                    )
-                    nc.vector.tensor_tensor(out=pre[:, cols], in0=acc[:], in1=bias[:, cols], op=ALU.add)
-                nc.gpsimd.tensor_scalar(
-                    out=pre[:, span], in0=pre[:, span], scalar1=FLT_MAX, scalar2=0.0, op0=ALU.min, op1=ALU.max
+        def finish(t, q):
+            first, rows = banks[q]
+            one = slice(t, t + 1)
+            if q == 0 and t + 2 < TOK_TILES:
+                turn(t + 2)
+            if q == 2 and t + 1 < TOK_TILES:
+                quantise_x(t + 1)
+            pre = flow.tile([P, BANK], F32, name="pre")
+            nc.vector.tensor_tensor(out=pre[:], in0=sums[q][:], in1=bias[:, first : first + BANK], op=ALU.add)
+            nc.gpsimd.tensor_scalar(out=pre[:], in0=pre[:], scalar1=FLT_MAX, scalar2=0.0, op0=ALU.min, op1=ALU.max)
+            enriched = flow.tile([P, BANK], F32, name="enriched")
+            nc.scalar.activation(out=enriched[:], in_=pre[:], func=ACT.Square)
+            if q == 0:
+                right[t] = enriched
+                fourth = flow.tile([P, BANK], BF16, name="fourth")
+                nc.scalar.activation(out=fourth[:], in_=enriched[:], func=ACT.Square, accum_out=norm2[:, one])
+            else:
+                nc.sync.dma_start(out=rows[:, t, :], in_=enriched[:])
+            if q == 2:
+                nc.gpsimd.tensor_scalar_max(out=norm2_floor[:, one], in0=norm2[:, one], scalar1=EPS_NORM * EPS_NORM)
+                nc.gpsimd.tensor_tensor(
+                    out=inv_norm[:, one], in0=norm2_floor[:, one], in1=minus_half[:, 0:1], op=ALU.pow
                 )
-                nc.scalar.activation(out=enriched[:, span], in_=pre[:, span], func=ACT.Square)
-                if rows is right_rows:
-                    fourth = flow.tile([P, HALF], BF16)
-                    nc.scalar.activation(
-                        out=fourth[:], in_=enriched[:, span], func=ACT.Square, accum_out=norm2[:, one]
-                    )
-                    nc.vector.tensor_scalar_max(out=norm2_floor[:, one], in0=norm2[:, one], scalar1=EPS_NORM * EPS_NORM)
-                    nc.scalar.activation(out=norm[:, one], in_=norm2_floor[:, one], func=ACT.Sqrt)
-                    nc.vector.reciprocal(out=inv_norm[:, one], in_=norm[:, one])
-                    unit = flow.tile([P, HALF], F32)
-                    nc.gpsimd.tensor_scalar(
-                        out=unit[:],
-                        in0=enriched[:, span],
-                        scalar1=inv_norm[:, one],
-                        scalar2=1.0,
-                        op0=ALU.mult,
-                        op1=ALU.mult,
-                    )
-                    nc.sync.dma_start(out=rows[:, i, :], in_=unit[:])
-                else:
-                    nc.sync.dma_start(out=rows[:, i, :], in_=enriched[:, span])
+                unit = flow.tile([P, BANK], F32, name="unit")
+                nc.scalar.activation(out=unit[:], in_=right[t][:], func=ACT.Copy, scale=inv_norm[:, one])
+                nc.sync.dma_start(out=banks[0][1][:, t, :], in_=unit[:])
 
-        normalise_pair(0)
-        for b in bank_order:
-            quantise_w_bank(b)
-        for j in range(PAIRS):
-            if j + 1 < PAIRS:
-                normalise_pair(j + 1)
-            enrich_tile(2 * j)
-            enrich_tile(2 * j + 1)
+        rms_statistics(0)
+        rms_statistics(1)
+        turn(0)
+        turn(1)
+        rms_statistics(2)
+        rms_statistics(3)
+        regroup_w(0)
+        quantise_x(0)
+        for u in range(UNITS + 1):
+            if u < UNITS:
+                if u < BANKS:
+                    quantise_w(u)
+                multiply(u // BANKS, u % BANKS)
+                if u + 1 < BANKS:
+                    regroup_w(u + 1)
+            if u >= 1:
+                finish((u - 1) // BANKS, (u - 1) % BANKS)

@@ -167,18 +167,28 @@ def tile_avey_pa_kernel(tc, x, g, W1, b1, out_0, out_1, out_2):
         inv_norm = keep.tile([P, TOK_TILES], F32)
         right = {}
 
-        def finish(t, q):
-            first, rows = banks[q]
-            one = slice(t, t + 1)
+        pre = {}
+
+        def add_bias(t, q):
+            first = banks[q][0]
             if q == 0 and t + 2 < TOK_TILES:
                 turn(t + 2)
             if q == 2 and t + 1 < TOK_TILES:
                 quantise_x(t + 1)
-            pre = flow.tile([P, BANK], F32, name="pre")
-            nc.vector.tensor_tensor(out=pre[:], in0=sums[q][:], in1=bias[:, first : first + BANK], op=ALU.add)
-            nc.gpsimd.tensor_scalar(out=pre[:], in0=pre[:], scalar1=FLT_MAX, scalar2=0.0, op0=ALU.min, op1=ALU.max)
+            pre[q] = flow.tile([P, BANK], F32, name="pre")
+            nc.vector.tensor_tensor(out=pre[q][:], in0=sums[q][:], in1=bias[:, first : first + BANK], op=ALU.add)
+
+        def enrich(t, q):
+            rows = banks[q][1]
+            one = slice(t, t + 1)
+            if q % 2 == 0:
+                nc.gpsimd.tensor_scalar(
+                    out=pre[q][:], in0=pre[q][:], scalar1=FLT_MAX, scalar2=0.0, op0=ALU.min, op1=ALU.max
+                )
+            else:
+                nc.vector.tensor_scalar_max(out=pre[q][:], in0=pre[q][:], scalar1=0.0)
             enriched = flow.tile([P, BANK], F32, name="enriched")
-            nc.scalar.activation(out=enriched[:], in_=pre[:], func=ACT.Square)
+            nc.scalar.activation(out=enriched[:], in_=pre[q][:], func=ACT.Square)
             if q == 0:
                 right[t] = enriched
                 fourth = flow.tile([P, BANK], BF16, name="fourth")
@@ -202,12 +212,14 @@ def tile_avey_pa_kernel(tc, x, g, W1, b1, out_0, out_1, out_2):
         rms_statistics(3)
         regroup_w(0)
         quantise_x(0)
-        for u in range(UNITS + 1):
+        for u in range(UNITS + 2):
             if u < UNITS:
                 if u < BANKS:
                     quantise_w(u)
                 multiply(u // BANKS, u % BANKS)
                 if u + 1 < BANKS:
                     regroup_w(u + 1)
-            if u >= 1:
-                finish((u - 1) // BANKS, (u - 1) % BANKS)
+            if 1 <= u <= UNITS:
+                add_bias((u - 1) // BANKS, (u - 1) % BANKS)
+            if u >= 2:
+                enrich((u - 2) // BANKS, (u - 2) % BANKS)

from contextlib import ExitStack

import concourse.masks as masks
import concourse.mybir as mybir

F32 = mybir.dt.float32
BF16 = mybir.dt.bfloat16
U32 = mybir.dt.uint32
U8 = mybir.dt.uint8
FP8X4 = mybir.dt.float8_e4m3fn_x4
ACT = mybir.ActivationFunctionType
ALU = mybir.AluOpType

P = 128
PACK = 4
TOKENS = 1024
D = 512
HEAD = 1024
HALF = 512
E = HEAD + HALF + HALF
BANK = 512
TOK_TILES = TOKENS // P
BANKS = E // BANK
UNITS = TOK_TILES * BANKS
EPS_RMS = 1e-6
EPS_NORM = 1e-12
FLT_MAX = 3.4028234663852886e38

FLOPS = 2 * TOKENS * D * E


def tile_avey_pa_kernel(tc, x, g, W1, b1, out_0, out_1, out_2):
    nc = tc.nc

    x_rows = x.flatten_outer_dims().rearrange("(p t) k -> p t k", t=TOK_TILES)
    head_rows = out_0.flatten_outer_dims().rearrange("(p t) f -> p t f", t=TOK_TILES)
    left_rows = out_1.flatten_outer_dims().rearrange("(p t) f -> p t f", t=TOK_TILES)
    right_rows = out_2.flatten_outer_dims().rearrange("(p t) f -> p t f", t=TOK_TILES)
    w_rows = W1.rearrange("(j p) f -> p j f", p=P)

    banks = (
        (HEAD + HALF, right_rows),
        (HEAD, left_rows),
        (0, head_rows[:, :, 0:BANK]),
        (BANK, head_rows[:, :, BANK:HEAD]),
    )

    with ExitStack() as ctx:
        ctx.enter_context(tc.manual_schedule())
        keep = ctx.enter_context(tc.tile_pool(name="keep", bufs=1))
        stage = ctx.enter_context(tc.tile_pool(name="stage", bufs=2))
        flow = ctx.enter_context(tc.tile_pool(name="flow", bufs=6))
        psum_gain = ctx.enter_context(tc.psum_pool(name="psum_gain", bufs=1))
        psum_turn = ctx.enter_context(tc.psum_pool(name="psum_turn", bufs=1))
        psum_acc = ctx.enter_context(tc.psum_pool(name="psum_acc", bufs=6))

        warm = keep.tile([P, 1], F32)
        nc.vector.memset(warm[:], 1.0)
        nc.scalar.activation(out=warm[:], in_=warm[:], func=ACT.Square)

        g_row = keep.tile([P, D], BF16)
        nc.vector.memset(g_row[:], 0.0)
        nc.scalar.dma_start(out=g_row[0:1, :], in_=g.unsqueeze(0))
        b_row = keep.tile([P, E], BF16)
        nc.vector.memset(b_row[:], 0.0)
        nc.scalar.dma_start(out=b_row[0:1, :], in_=b1.unsqueeze(0))
        ones = keep.tile([P, P], BF16)
        nc.vector.memset(ones[:], 1.0)
        ident = keep.tile([P, P], BF16)
        masks.make_identity(nc, ident[:])
        minus_half = keep.tile([P, 2], F32)
        nc.gpsimd.memset(minus_half[:], -0.5)

        x_sb = keep.tile([P, TOK_TILES, D], BF16)
        nc.sync.dma_start(out=x_sb[:, 0:2, :], in_=x_rows[:, 0:2, :])
        nc.sync.dma_start(out=x_sb[:, 2:TOK_TILES, :], in_=x_rows[:, 2:TOK_TILES, :])
        w_raw = keep.tile([P, PACK, E], BF16)
        for first, rows in banks:
            nc.sync.dma_start(out=w_raw[:, :, first : first + BANK], in_=w_rows[:, :, first : first + BANK])

        gain = psum_gain.tile([P, D], F32)
        nc.tensor.matmul(out=gain[:], lhsT=ones[:], rhs=g_row[:], start=True, stop=True)
        bias = keep.tile([P, E], F32)
        for first, rows in banks:
            spread = psum_acc.tile([P, BANK], F32, tag="acc")
            nc.tensor.matmul(out=spread[:], lhsT=ones[:], rhs=b_row[:, first : first + BANK], start=True, stop=True)
            nc.vector.tensor_copy(out=bias[:, first : first + BANK], in_=spread[:])

        x_codes = keep.tile([P, TOKENS], U32, align_bytes=64)
        x_scales = keep.tile([P, TOKENS], U8, align_bytes=64)
        w_codes = keep.tile([P, E], U32, align_bytes=64)
        w_scales = keep.tile([P, E], U8, align_bytes=64)

        squares = keep.tile([P, TOK_TILES, D], BF16)
        sumsq = keep.tile([P, TOK_TILES], F32)
        mean_sq = keep.tile([P, TOK_TILES], F32)
        rstd = keep.tile([P, TOK_TILES], F32)

        def rms_statistics(pair):
            both = slice(2 * pair, 2 * pair + 2)
            for t in (2 * pair, 2 * pair + 1):
                nc.scalar.activation(
                    out=squares[:, t, :], in_=x_sb[:, t, :], func=ACT.Square, accum_out=sumsq[:, t : t + 1]
                )
            nc.gpsimd.tensor_scalar(
                out=mean_sq[:, both], in0=sumsq[:, both], scalar1=1.0 / D, scalar2=EPS_RMS, op0=ALU.mult, op1=ALU.add
            )
            nc.gpsimd.tensor_tensor(out=rstd[:, both], in0=mean_sq[:, both], in1=minus_half[:], op=ALU.pow)

        x_grouped = {}

        def turn(t):
            xn = stage.tile([P, D], BF16, name="xn")
            nc.vector.scalar_tensor_tensor(
                out=xn[:], in0=x_sb[:, t, :], scalar=rstd[:, t : t + 1], in1=gain[:], op0=ALU.mult, op1=ALU.mult
            )
            turned = psum_turn.tile([P, PACK, P], BF16, name="turned")
            for j in range(PACK):
                nc.tensor.transpose(turned[:, j, :], xn[:, j * P : (j + 1) * P], ident[:])
            x_grouped[t] = stage.tile([P, P, PACK], BF16, align_bytes=64, name="x_grouped")
            nc.scalar.copy(out=x_grouped[t][:], in_=turned[:].rearrange("p j r -> p r j"))

        def quantise_x(t):
            toks = slice(t * P, (t + 1) * P)
            nc.vector.quantize_mx(
                out=x_codes[:, toks].bitcast(FP8X4),
                scales=x_scales[:, toks],
                in_=x_grouped[t][:].rearrange("p r j -> p (r j)"),
            )

        w_grouped = {}

        def regroup_w(q):
            first = banks[q][0]
            w_grouped[q] = stage.tile([P, BANK, PACK], BF16, align_bytes=64, name="w_grouped")
            nc.vector.tensor_copy(
                out=w_grouped[q][:].rearrange("p (c i) j -> p c j i", i=4),
                in_=w_raw[:, :, first : first + BANK].rearrange("p j (c i) -> p c j i", i=4),
            )

        def quantise_w(q):
            first = banks[q][0]
            nc.vector.quantize_mx(
                out=w_codes[:, first : first + BANK].bitcast(FP8X4),
                scales=w_scales[:, first : first + BANK],
                in_=w_grouped[q][:].rearrange("p f j -> p (f j)"),
            )

        sums = {}

        def multiply(t, q):
            first = banks[q][0]
            toks = slice(t * P, (t + 1) * P)
            sums[q] = psum_acc.tile([P, BANK], F32, tag="acc", name="acc")
            nc.tensor.matmul_mx(
                out=sums[q][:],
                lhsT=x_codes[:, toks].bitcast(FP8X4),
                lhsT_scale=x_scales[:, toks],
                rhs=w_codes[:, first : first + BANK].bitcast(FP8X4),
                rhs_scale=w_scales[:, first : first + BANK],
                start=True,
                stop=True,
            )

        norm2 = keep.tile([P, TOK_TILES], F32)
        norm2_floor = keep.tile([P, TOK_TILES], F32)
        inv_norm = keep.tile([P, TOK_TILES], F32)
        right = {}

        pre = {}

        def add_bias(t, q):
            first = banks[q][0]
            if q == 0 and t + 2 < TOK_TILES:
                turn(t + 2)
            if q == 2 and t + 1 < TOK_TILES:
                quantise_x(t + 1)
            pre[q] = flow.tile([P, BANK], F32, name="pre")
            nc.vector.tensor_tensor(out=pre[q][:], in0=sums[q][:], in1=bias[:, first : first + BANK], op=ALU.add)

        def enrich(t, q):
            rows = banks[q][1]
            one = slice(t, t + 1)
            if q % 2 == 0:
                nc.gpsimd.tensor_scalar(
                    out=pre[q][:], in0=pre[q][:], scalar1=FLT_MAX, scalar2=0.0, op0=ALU.min, op1=ALU.max
                )
            else:
                nc.vector.tensor_scalar_max(out=pre[q][:], in0=pre[q][:], scalar1=0.0)
            enriched = flow.tile([P, BANK], F32, name="enriched")
            nc.scalar.activation(out=enriched[:], in_=pre[q][:], func=ACT.Square)
            if q == 0:
                right[t] = enriched
                fourth = flow.tile([P, BANK], BF16, name="fourth")
                nc.scalar.activation(out=fourth[:], in_=enriched[:], func=ACT.Square, accum_out=norm2[:, one])
            else:
                nc.sync.dma_start(out=rows[:, t, :], in_=enriched[:])
            if q == 2:
                nc.gpsimd.tensor_scalar_max(out=norm2_floor[:, one], in0=norm2[:, one], scalar1=EPS_NORM * EPS_NORM)
                nc.gpsimd.tensor_tensor(
                    out=inv_norm[:, one], in0=norm2_floor[:, one], in1=minus_half[:, 0:1], op=ALU.pow
                )
                unit = flow.tile([P, BANK], F32, name="unit")
                nc.scalar.activation(out=unit[:], in_=right[t][:], func=ACT.Copy, scale=inv_norm[:, one])
                nc.sync.dma_start(out=banks[0][1][:, t, :], in_=unit[:])

        rms_statistics(0)
        rms_statistics(1)
        turn(0)
        turn(1)
        rms_statistics(2)
        rms_statistics(3)
        regroup_w(0)
        quantise_x(0)
        for u in range(UNITS + 2):
            if u < UNITS:
                if u < BANKS:
                    quantise_w(u)
                multiply(u // BANKS, u % BANKS)
                if u + 1 < BANKS:
                    regroup_w(u + 1)
            if 1 <= u <= UNITS:
                add_bias((u - 1) // BANKS, (u - 1) % BANKS)
            if u >= 2:
                enrich((u - 2) // BANKS, (u - 2) % BANKS)
